import numpy as np
import ml_dtypes

BF16 = ml_dtypes.bfloat16


def bf(x):
    return np.asarray(x, np.float32).astype(BF16)


def f32(x):
    return np.asarray(x, np.float32)


def f64(x):
    return np.asarray(x).astype(np.float64)


def striped(idx):
    return np.tile(idx.reshape(-1, 16).T, (8, 1))


C, S, R, NV, MC, N = 256, 2048, 2, 128, 32, 4096
DAYS = 180.0
SPAN = 365.0


def setup_inputs():
    return {"table": f32(np.random.standard_normal((C, S))), "deltas": f32(SPAN * np.random.uniform(size=(1, NV))), "tf_w": f32(np.random.standard_normal((C, 1))), "tf_b": f32(0.1 * np.random.standard_normal((C, 1))), "tp_w": bf(np.random.standard_normal((C, C)) / np.sqrt(C)), "tp_b": f32(0.1 * np.random.standard_normal((C, 1))), "offs": striped(np.concatenate([np.random.permutation(S) for _ in range(R)]))}


def reference(table, deltas, tf_w, tf_b, tp_w, tp_b, offs):
    idx = offs[:16].T.reshape(-1)
    picked = f64(table)[:, idx].reshape(C, NV, MC)
    vis = picked.sum(axis=2) / MC
    freq = f64(tf_w) * (f64(deltas) / DAYS) + f64(tf_b)
    u = 1.0 - np.tanh(freq) ** 2
    te = f64(tp_w).T @ u + f64(tp_b)
    return vis + te

@@ -1,0 +1,81 @@
+import concourse.mybir as mybir
+
+F32, BF16, U16 = mybir.dt.float32, mybir.dt.bfloat16, mybir.dt.uint16
+ACT = mybir.ActivationFunctionType
+ALU = mybir.AluOpType
+
+P = 128
+C = 256
+S = 2048
+NV = 128
+MC = 32
+N = NV * MC
+DAYS = 180.0
+BLOCKS = C // P
+PIECE = 2048
+PIECE_VISITS = PIECE // MC
+
+FLOPS = 2 * C * C * NV
+
+
+def tile_graphhyperbolicvisitencoderglobal_kernel(tc, table, deltas, tf_w, tf_b, tp_w, tp_b, offs, out):
+    nc = tc.nc
+    with (
+        tc.tile_pool(name="held", bufs=1) as held,
+        tc.tile_pool(name="ring", bufs=3) as ring,
+        tc.psum_pool(name="psum", bufs=1) as psum,
+    ):
+        offsets = held.tile([P, N // 16], U16, name="offsets")
+        nc.sync.dma_start(offsets[:], offs)
+        tables = [held.tile([P, S], F32, name=f"table{b}") for b in range(BLOCKS)]
+        for b in range(BLOCKS):
+            nc.sync.dma_start(tables[b][:], table[b * P : (b + 1) * P, :])
+
+        slope_bias = held.tile([2, C], F32, name="slope_bias")
+        gap_days = held.tile([2, NV], F32, name="gap_days")
+        nc.vector.memset(gap_days[:], DAYS)
+        nc.scalar.dma_start(slope_bias[0:1, :], tf_w.rearrange("c o -> o c"))
+        nc.scalar.dma_start(slope_bias[1:2, :], tf_b.rearrange("c o -> o c"))
+        nc.scalar.dma_start(gap_days[0:1, :], deltas)
+        weights = held.tile([P, BLOCKS, C], BF16, name="weights")
+        nc.gpsimd.dma_start(weights[:], tp_w.rearrange("(db p) c -> p db c", p=P))
+        out_bias = held.tile([1, C], F32, name="out_bias")
+        nc.gpsimd.dma_start(out_bias[:], tp_b.rearrange("c o -> o c"))
+        ones = held.tile([1, NV], F32, name="ones")
+        nc.vector.memset(ones[:], 1.0)
+
+        freq180 = psum.tile([P, BLOCKS * NV], F32, name="freq180")
+        for db in range(BLOCKS):
+            nc.tensor.matmul(
+                freq180[:, db * NV : (db + 1) * NV], slope_bias[:, db * P : (db + 1) * P], gap_days[:],
+                start=True, stop=True,
+            )
+        tanh = held.tile([P, BLOCKS * NV], F32, name="tanh")
+        nc.scalar.activation(tanh[:], freq180[:], ACT.Tanh, scale=1.0 / DAYS)
+        squared = held.tile([P, BLOCKS * NV], F32, name="squared")
+        nc.vector.tensor_tensor(squared[:], tanh[:], tanh[:], ALU.mult)
+        u = held.tile([P, BLOCKS * NV], BF16, name="u")
+        nc.vector.tensor_scalar(u[:], squared[:], -1.0, 1.0, ALU.mult, ALU.add)
+        te = [psum.tile([P, NV], F32, name=f"te{cb}") for cb in range(BLOCKS)]
+        for cb in range(BLOCKS):
+            for db in range(BLOCKS):
+                nc.tensor.matmul(
+                    te[cb][:], weights[:, db, cb * P : (cb + 1) * P], u[:, db * NV : (db + 1) * NV],
+                    start=(db == 0), stop=False,
+                )
+            nc.tensor.matmul(te[cb][:], out_bias[:, cb * P : (cb + 1) * P], ones[:], start=False, stop=True)
+
+        for b in range(BLOCKS):
+            sums = held.tile([P, NV], F32, name=f"sums{b}")
+            for k in range(N // PIECE):
+                picked = ring.tile([P, PIECE], F32, name="picked")
+                piece_offsets = offsets[:, k * (PIECE // 16) : (k + 1) * (PIECE // 16)]
+                nc.scalar.activation(picked[:], tables[b][:].indirect(piece_offsets), ACT.Copy)
+                nc.vector.tensor_reduce(
+                    sums[:, k * PIECE_VISITS : (k + 1) * PIECE_VISITS],
+                    picked[:].rearrange("p (n m) -> p n m", m=MC),
+                    mybir.AxisListType.X, ALU.add,
+                )
+            result = held.tile([P, NV], F32, name=f"result{b}")
+            nc.vector.scalar_tensor_tensor(result[:], sums[:], 1.0 / MC, te[b][:], ALU.mult, ALU.add)
+            nc.sync.dma_start(out[b * P : (b + 1) * P, :], result[:])

@@ -25,22 +25,21 @@ def tile_graphhyperbolicvisitencoderglobal_kernel(tc, table, deltas, tf_w, tf_b,
         tc.tile_pool(name="ring", bufs=3) as ring,
         tc.psum_pool(name="psum", bufs=1) as psum,
     ):
+        slope_bias = held.tile([2, C], F32, name="slope_bias")
+        gap_days = held.tile([2, NV], F32, name="gap_days")
+        nc.vector.memset(gap_days[:], DAYS)
+        nc.sync.dma_start(slope_bias[0:1, :], tf_w.rearrange("c o -> o c"))
+        nc.sync.dma_start(slope_bias[1:2, :], tf_b.rearrange("c o -> o c"))
+        nc.sync.dma_start(gap_days[0:1, :], deltas)
         offsets = held.tile([P, N // 16], U16, name="offsets")
         nc.sync.dma_start(offsets[:], offs)
         tables = [held.tile([P, S], F32, name=f"table{b}") for b in range(BLOCKS)]
         for b in range(BLOCKS):
             nc.sync.dma_start(tables[b][:], table[b * P : (b + 1) * P, :])
-
-        slope_bias = held.tile([2, C], F32, name="slope_bias")
-        gap_days = held.tile([2, NV], F32, name="gap_days")
-        nc.vector.memset(gap_days[:], DAYS)
-        nc.scalar.dma_start(slope_bias[0:1, :], tf_w.rearrange("c o -> o c"))
-        nc.scalar.dma_start(slope_bias[1:2, :], tf_b.rearrange("c o -> o c"))
-        nc.scalar.dma_start(gap_days[0:1, :], deltas)
         weights = held.tile([P, BLOCKS, C], BF16, name="weights")
-        nc.gpsimd.dma_start(weights[:], tp_w.rearrange("(db p) c -> p db c", p=P))
+        nc.scalar.dma_start(weights[:], tp_w.rearrange("(db p) c -> p db c", p=P))
         out_bias = held.tile([1, C], F32, name="out_bias")
-        nc.gpsimd.dma_start(out_bias[:], tp_b.rearrange("c o -> o c"))
+        nc.scalar.dma_start(out_bias[:], tp_b.rearrange("c o -> o c"))
         ones = held.tile([1, NV], F32, name="ones")
         nc.vector.memset(ones[:], 1.0)
 

@@ -12,7 +12,7 @@ MC = 32
 N = NV * MC
 DAYS = 180.0
 BLOCKS = C // P
-PIECE = 2048
+PIECE = 512
 PIECE_VISITS = PIECE // MC
 
 FLOPS = 2 * C * C * NV

@@ -12,10 +12,19 @@ MC = 32
 N = NV * MC
 DAYS = 180.0
 BLOCKS = C // P
-PIECE = 512
-PIECE_VISITS = PIECE // MC
+LONGEST = S
+SHORTEST = 256
 
 FLOPS = 2 * C * C * NV
+
+
+def pieces():
+    cut, done = [], 0
+    while done < BLOCKS * N:
+        length = min(LONGEST, max(SHORTEST, (BLOCKS * N - done) // 2))
+        cut.append((done // N, done % N, done % N + length))
+        done += length
+    return cut
 
 
 def tile_graphhyperbolicvisitencoderglobal_kernel(tc, table, deltas, tf_w, tf_b, tp_w, tp_b, offs, out):
@@ -25,12 +34,12 @@ def tile_graphhyperbolicvisitencoderglobal_kernel(tc, table, deltas, tf_w, tf_b,
         tc.tile_pool(name="ring", bufs=3) as ring,
         tc.psum_pool(name="psum", bufs=1) as psum,
     ):
-        slope_bias = held.tile([2, C], F32, name="slope_bias")
-        gap_days = held.tile([2, NV], F32, name="gap_days")
-        nc.vector.memset(gap_days[:], DAYS)
-        nc.sync.dma_start(slope_bias[0:1, :], tf_w.rearrange("c o -> o c"))
-        nc.sync.dma_start(slope_bias[1:2, :], tf_b.rearrange("c o -> o c"))
-        nc.sync.dma_start(gap_days[0:1, :], deltas)
+        bias_slope = held.tile([2, C], F32, name="bias_slope")
+        days_gap = held.tile([2, NV], F32, name="days_gap")
+        nc.vector.memset(days_gap[0:1, :], DAYS)
+        nc.sync.dma_start(bias_slope[0:1, :], tf_b.rearrange("c o -> o c"))
+        nc.sync.dma_start(bias_slope[1:2, :], tf_w.rearrange("c o -> o c"))
+        nc.sync.dma_start(days_gap[1:2, :], deltas)
         offsets = held.tile([P, N // 16], U16, name="offsets")
         nc.sync.dma_start(offsets[:], offs)
         tables = [held.tile([P, S], F32, name=f"table{b}") for b in range(BLOCKS)]
@@ -46,7 +55,7 @@ def tile_graphhyperbolicvisitencoderglobal_kernel(tc, table, deltas, tf_w, tf_b,
         freq180 = psum.tile([P, BLOCKS * NV], F32, name="freq180")
         for db in range(BLOCKS):
             nc.tensor.matmul(
-                freq180[:, db * NV : (db + 1) * NV], slope_bias[:, db * P : (db + 1) * P], gap_days[:],
+                freq180[:, db * NV : (db + 1) * NV], bias_slope[:, db * P : (db + 1) * P], days_gap[:],
                 start=True, stop=True,
             )
         tanh = held.tile([P, BLOCKS * NV], F32, name="tanh")
@@ -64,17 +73,21 @@ def tile_graphhyperbolicvisitencoderglobal_kernel(tc, table, deltas, tf_w, tf_b,
                 )
             nc.tensor.matmul(te[cb][:], out_bias[:, cb * P : (cb + 1) * P], ones[:], start=False, stop=True)
 
-        for b in range(BLOCKS):
-            sums = held.tile([P, NV], F32, name=f"sums{b}")
-            for k in range(N // PIECE):
-                picked = ring.tile([P, PIECE], F32, name="picked")
-                piece_offsets = offsets[:, k * (PIECE // 16) : (k + 1) * (PIECE // 16)]
-                nc.scalar.activation(picked[:], tables[b][:].indirect(piece_offsets), ACT.Copy)
-                nc.vector.tensor_reduce(
-                    sums[:, k * PIECE_VISITS : (k + 1) * PIECE_VISITS],
-                    picked[:].rearrange("p (n m) -> p n m", m=MC),
-                    mybir.AxisListType.X, ALU.add,
-                )
-            result = held.tile([P, NV], F32, name=f"result{b}")
-            nc.vector.scalar_tensor_tensor(result[:], sums[:], 1.0 / MC, te[b][:], ALU.mult, ALU.add)
-            nc.sync.dma_start(out[b * P : (b + 1) * P, :], result[:])
+        sums = [held.tile([P, NV], F32, name=f"sums{b}") for b in range(BLOCKS)]
+        result = [held.tile([P, NV], F32, name=f"result{b}") for b in range(BLOCKS)]
+        for b, first, end in pieces():
+            picked = ring.tile([P, LONGEST], F32, name="picked")
+            nc.scalar.activation(
+                picked[:, : end - first], tables[b][:].indirect(offsets[:, first // 16 : end // 16]), ACT.Copy
+            )
+            visits = slice(first // MC, end // MC)
+            nc.vector.tensor_reduce(
+                sums[b][:, visits],
+                picked[:, : end - first].rearrange("p (n m) -> p n m", m=MC),
+                mybir.AxisListType.X, ALU.add,
+            )
+            nc.vector.scalar_tensor_tensor(
+                result[b][:, visits], sums[b][:, visits], 1.0 / MC, te[b][:, visits], ALU.mult, ALU.add
+            )
+            if end == N:
+                nc.sync.dma_start(out[b * P : (b + 1) * P, :], result[b][:])

@@ -89,5 +89,4 @@ def tile_graphhyperbolicvisitencoderglobal_kernel(tc, table, deltas, tf_w, tf_b,
             nc.vector.scalar_tensor_tensor(
                 result[b][:, visits], sums[b][:, visits], 1.0 / MC, te[b][:, visits], ALU.mult, ALU.add
             )
-            if end == N:
-                nc.sync.dma_start(out[b * P : (b + 1) * P, :], result[b][:])
+            nc.sync.dma_start(out[b * P : (b + 1) * P, visits], result[b][:, visits])

@@ -46,9 +46,9 @@ def tile_graphhyperbolicvisitencoderglobal_kernel(tc, table, deltas, tf_w, tf_b,
         for b in range(BLOCKS):
             nc.sync.dma_start(tables[b][:], table[b * P : (b + 1) * P, :])
         weights = held.tile([P, BLOCKS, C], BF16, name="weights")
-        nc.scalar.dma_start(weights[:], tp_w.rearrange("(db p) c -> p db c", p=P))
+        nc.sync.dma_start(weights[:], tp_w.rearrange("(db p) c -> p db c", p=P))
         out_bias = held.tile([1, C], F32, name="out_bias")
-        nc.scalar.dma_start(out_bias[:], tp_b.rearrange("c o -> o c"))
+        nc.sync.dma_start(out_bias[:], tp_b.rearrange("c o -> o c"))
         ones = held.tile([1, NV], F32, name="ones")
         nc.vector.memset(ones[:], 1.0)
 

@@ -37,8 +37,8 @@ def tile_graphhyperbolicvisitencoderglobal_kernel(tc, table, deltas, tf_w, tf_b,
         bias_slope = held.tile([2, C], F32, name="bias_slope")
         days_gap = held.tile([2, NV], F32, name="days_gap")
         nc.vector.memset(days_gap[0:1, :], DAYS)
-        nc.sync.dma_start(bias_slope[0:1, :], tf_b.rearrange("c o -> o c"))
-        nc.sync.dma_start(bias_slope[1:2, :], tf_w.rearrange("c o -> o c"))
+        nc.scalar.dma_start(bias_slope[0:1, :], tf_b.rearrange("c o -> o c"))
+        nc.scalar.dma_start(bias_slope[1:2, :], tf_w.rearrange("c o -> o c"))
         nc.sync.dma_start(days_gap[1:2, :], deltas)
         offsets = held.tile([P, N // 16], U16, name="offsets")
         nc.sync.dma_start(offsets[:], offs)

@@ -13,18 +13,16 @@ N = NV * MC
 DAYS = 180.0
 BLOCKS = C // P
 LONGEST = S
-SHORTEST = 256
+STORE = 8
 
 FLOPS = 2 * C * C * NV
 
 
-def pieces():
-    cut, done = [], 0
-    while done < BLOCKS * N:
-        length = min(LONGEST, max(SHORTEST, (BLOCKS * N - done) // 2))
-        cut.append((done // N, done % N, done % N + length))
-        done += length
-    return cut
+def block_cuts():
+    cuts = [[first for first in range(0, N + 1, LONGEST)] for b in range(BLOCKS)]
+    part = LONGEST // 15 // MC * MC
+    cuts[-1] += [N - 7 * part, N - 3 * part, N - part]
+    return [sorted(c) for c in cuts]
 
 
 def tile_graphhyperbolicvisitencoderglobal_kernel(tc, table, deltas, tf_w, tf_b, tp_w, tp_b, offs, out):
@@ -75,18 +73,28 @@ def tile_graphhyperbolicvisitencoderglobal_kernel(tc, table, deltas, tf_w, tf_b,
 
         sums = [held.tile([P, NV], F32, name=f"sums{b}") for b in range(BLOCKS)]
         result = [held.tile([P, NV], F32, name=f"result{b}") for b in range(BLOCKS)]
-        for b, first, end in pieces():
-            picked = ring.tile([P, LONGEST], F32, name="picked")
-            nc.scalar.activation(
-                picked[:, : end - first], tables[b][:].indirect(offsets[:, first // 16 : end // 16]), ACT.Copy
-            )
-            visits = slice(first // MC, end // MC)
-            nc.vector.tensor_reduce(
-                sums[b][:, visits],
-                picked[:, : end - first].rearrange("p (n m) -> p n m", m=MC),
-                mybir.AxisListType.X, ALU.add,
-            )
+
+        def means_and_store(b, start, stop):
+            visits = slice(start, stop)
             nc.vector.scalar_tensor_tensor(
                 result[b][:, visits], sums[b][:, visits], 1.0 / MC, te[b][:, visits], ALU.mult, ALU.add
             )
             nc.sync.dma_start(out[b * P : (b + 1) * P, visits], result[b][:, visits])
+
+        for b, cuts in enumerate(block_cuts()):
+            stored = 0
+            for first, end in zip(cuts[:-1], cuts[1:]):
+                picked = ring.tile([P, LONGEST], F32, name="picked")
+                nc.scalar.activation(
+                    picked[:, : end - first], tables[b][:].indirect(offsets[:, first // 16 : end // 16]), ACT.Copy
+                )
+                nc.vector.tensor_reduce(
+                    sums[b][:, first // MC : end // MC],
+                    picked[:, : end - first].rearrange("p (n m) -> p n m", m=MC),
+                    mybir.AxisListType.X, ALU.add,
+                )
+                summed_before = first // MC // STORE * STORE
+                if summed_before > stored:
+                    means_and_store(b, stored, summed_before)
+                    stored = summed_before
+            means_and_store(b, stored, NV)

@@ -93,8 +93,9 @@ def tile_graphhyperbolicvisitencoderglobal_kernel(tc, table, deltas, tf_w, tf_b,
                     picked[:, : end - first].rearrange("p (n m) -> p n m", m=MC),
                     mybir.AxisListType.X, ALU.add,
                 )
-                summed_before = first // MC // STORE * STORE
-                if summed_before > stored:
-                    means_and_store(b, stored, summed_before)
-                    stored = summed_before
-            means_and_store(b, stored, NV)
+                ready = (end if end - first == LONGEST else first) // MC // STORE * STORE
+                if end < N or b < BLOCKS - 1:
+                    if ready > stored:
+                        means_and_store(b, stored, ready)
+                    stored = ready
+        means_and_store(BLOCKS - 1, stored, NV)

import concourse.mybir as mybir

F32, BF16, U16 = mybir.dt.float32, mybir.dt.bfloat16, mybir.dt.uint16
ACT = mybir.ActivationFunctionType
ALU = mybir.AluOpType

P = 128
C = 256
S = 2048
NV = 128
MC = 32
N = NV * MC
DAYS = 180.0
BLOCKS = C // P
LONGEST = S
STORE = 8

FLOPS = 2 * C * C * NV


def block_cuts():
    cuts = [[first for first in range(0, N + 1, LONGEST)] for b in range(BLOCKS)]
    part = LONGEST // 15 // MC * MC
    cuts[-1] += [N - 7 * part, N - 3 * part, N - part]
    return [sorted(c) for c in cuts]


def tile_graphhyperbolicvisitencoderglobal_kernel(tc, table, deltas, tf_w, tf_b, tp_w, tp_b, offs, out):
    nc = tc.nc
    with (
        tc.tile_pool(name="held", bufs=1) as held,
        tc.tile_pool(name="ring", bufs=3) as ring,
        tc.psum_pool(name="psum", bufs=1) as psum,
    ):
        bias_slope = held.tile([2, C], F32, name="bias_slope")
        days_gap = held.tile([2, NV], F32, name="days_gap")
        nc.vector.memset(days_gap[0:1, :], DAYS)
        nc.scalar.dma_start(bias_slope[0:1, :], tf_b.rearrange("c o -> o c"))
        nc.scalar.dma_start(bias_slope[1:2, :], tf_w.rearrange("c o -> o c"))
        nc.sync.dma_start(days_gap[1:2, :], deltas)
        offsets = held.tile([P, N // 16], U16, name="offsets")
        nc.sync.dma_start(offsets[:], offs)
        tables = [held.tile([P, S], F32, name=f"table{b}") for b in range(BLOCKS)]
        for b in range(BLOCKS):
            nc.sync.dma_start(tables[b][:], table[b * P : (b + 1) * P, :])
        weights = held.tile([P, BLOCKS, C], BF16, name="weights")
        nc.sync.dma_start(weights[:], tp_w.rearrange("(db p) c -> p db c", p=P))
        out_bias = held.tile([1, C], F32, name="out_bias")
        nc.sync.dma_start(out_bias[:], tp_b.rearrange("c o -> o c"))
        ones = held.tile([1, NV], F32, name="ones")
        nc.vector.memset(ones[:], 1.0)

        freq180 = psum.tile([P, BLOCKS * NV], F32, name="freq180")
        for db in range(BLOCKS):
            nc.tensor.matmul(
                freq180[:, db * NV : (db + 1) * NV], bias_slope[:, db * P : (db + 1) * P], days_gap[:],
                start=True, stop=True,
            )
        tanh = held.tile([P, BLOCKS * NV], F32, name="tanh")
        nc.scalar.activation(tanh[:], freq180[:], ACT.Tanh, scale=1.0 / DAYS)
        squared = held.tile([P, BLOCKS * NV], F32, name="squared")
        nc.vector.tensor_tensor(squared[:], tanh[:], tanh[:], ALU.mult)
        u = held.tile([P, BLOCKS * NV], BF16, name="u")
        nc.vector.tensor_scalar(u[:], squared[:], -1.0, 1.0, ALU.mult, ALU.add)
        te = [psum.tile([P, NV], F32, name=f"te{cb}") for cb in range(BLOCKS)]
        for cb in range(BLOCKS):
            for db in range(BLOCKS):
                nc.tensor.matmul(
                    te[cb][:], weights[:, db, cb * P : (cb + 1) * P], u[:, db * NV : (db + 1) * NV],
                    start=(db == 0), stop=False,
                )
            nc.tensor.matmul(te[cb][:], out_bias[:, cb * P : (cb + 1) * P], ones[:], start=False, stop=True)

        sums = [held.tile([P, NV], F32, name=f"sums{b}") for b in range(BLOCKS)]
        result = [held.tile([P, NV], F32, name=f"result{b}") for b in range(BLOCKS)]

        def means_and_store(b, start, stop):
            visits = slice(start, stop)
            nc.vector.scalar_tensor_tensor(
                result[b][:, visits], sums[b][:, visits], 1.0 / MC, te[b][:, visits], ALU.mult, ALU.add
            )
            nc.sync.dma_start(out[b * P : (b + 1) * P, visits], result[b][:, visits])

        for b, cuts in enumerate(block_cuts()):
            stored = 0
            for first, end in zip(cuts[:-1], cuts[1:]):
                picked = ring.tile([P, LONGEST], F32, name="picked")
                nc.scalar.activation(
                    picked[:, : end - first], tables[b][:].indirect(offsets[:, first // 16 : end // 16]), ACT.Copy
                )
                nc.vector.tensor_reduce(
                    sums[b][:, first // MC : end // MC],
                    picked[:, : end - first].rearrange("p (n m) -> p n m", m=MC),
                    mybir.AxisListType.X, ALU.add,
                )
                ready = (end if end - first == LONGEST else first) // MC // STORE * STORE
                if end < N or b < BLOCKS - 1:
                    if ready > stored:
                        means_and_store(b, stored, ready)
                    stored = ready
        means_and_store(BLOCKS - 1, stored, NV)
